import numpy as np
import ml_dtypes


def mxq(x, axis, fmt="e4m3"):
    dtype, down = {"e4m3": (ml_dtypes.float8_e4m3fn, 7), "e5m2": (ml_dtypes.float8_e5m2, 14)}[fmt]
    v = np.moveaxis(np.asarray(x, np.float32).astype(ml_dtypes.bfloat16).astype(np.float64), axis, -1)
    blocks = v.reshape(v.shape[:-1] + (-1, 32))
    amax = np.abs(blocks).max(-1, keepdims=True)
    byte = np.maximum(np.where(amax > 0, np.frexp(amax)[1] - 1 + 127, 0) - down, 1)
    scale = np.exp2(byte - 127.0)
    codes = (blocks / scale).astype(np.float32).astype(dtype).astype(np.float64)
    return np.moveaxis((codes * scale).reshape(v.shape), -1, axis)


WIDE = False


def mx_kscale(k):
    if not WIDE:
        return np.ones(k)
    levels = np.array([10, -10, 5, -5, 0])
    if k % 512:
        return np.exp2(np.random.permutation(np.resize(levels, k // 32))).repeat(32)
    a = np.empty((k // 512, 16))
    for p in range(k // 512):
        a[p, :8] = np.random.permutation(np.resize(levels, 8))
        for g in range(8):
            far = levels[np.abs(levels - a[p, g]) >= 10]
            a[p, g + 8] = far[np.random.randint(len(far))]
    return np.exp2(a.ravel()).repeat(32)


BF16 = ml_dtypes.bfloat16


def bf(x):
    return np.asarray(x, np.float32).astype(BF16)


def f64(x):
    return np.asarray(x).astype(np.float64)


B, C, HH, WW = 32, 512, 16, 16
N = HH * WW


def setup_inputs():
    s, t = mx_kscale(C), mx_kscale(C)
    return {"x": bf(np.random.standard_normal((B, C, HH, WW)) * s[None, :, None, None]),
            "Wq": bf(np.random.standard_normal((C, C)) * 1.4 / np.sqrt(C) * t[:, None] / s[None, :]),
            "bq": bf(np.random.standard_normal(C) * 0.2 * t),
            "k": bf(np.random.standard_normal((B, N, C)) * 1.4 / t)}


def reference(x, Wq, bq, k):
    xt = f64(x).reshape(B, C, N)
    q = (mxq(xt, 1, "e4m3").transpose(0, 2, 1) @ mxq(f64(Wq), 1, "e4m3").T) + f64(bq)
    scores = mxq(q / np.sqrt(C), 2, "e4m3") @ mxq(f64(k), 2, "e4m3").transpose(0, 2, 1)
    e = np.exp(scores - scores.max(-1, keepdims=True))
    return e / e.sum(-1, keepdims=True)

@@ -1,0 +1,279 @@
+import math
+from contextlib import ExitStack
+
+import concourse.mybir as mybir
+from concourse.masks import make_identity
+
+F32 = mybir.dt.float32
+BF16 = mybir.dt.bfloat16
+U32 = mybir.dt.uint32
+U8 = mybir.dt.uint8
+FP8X4 = mybir.dt.float8_e4m3fn_x4
+ACT = mybir.ActivationFunctionType
+ALU = mybir.AluOpType
+
+P = 128
+PACK = 4
+BATCHES = 32
+CHANNELS = P * PACK
+TOKENS = 256
+KEYS = 256
+HALVES = TOKENS // P
+PAIR = 2
+STEPS = BATCHES // PAIR
+COLS = PAIR * TOKENS
+ROW_TILES = PAIR * HALVES
+RUN = 4
+Q_SCALE = 1.0 / math.sqrt(CHANNELS)
+
+PROJECT_LAG = 1
+SCORE_LAG = 2
+SOFTMAX_LAG = 3
+NORM_LAG = 4
+LOOKAHEAD = 3
+
+FLOPS = 2 * BATCHES * TOKENS * CHANNELS * CHANNELS + 2 * BATCHES * TOKENS * KEYS * CHANNELS
+
+
+def tile_visionattention_pa_t_kernel(tc, x, Wq, bq, k, out):
+    nc = tc.nc
+    with ExitStack() as ctx:
+        const = ctx.enter_context(tc.tile_pool(name="const", bufs=1))
+        rows = ctx.enter_context(tc.tile_pool(name="rows", bufs=LOOKAHEAD + 1 + PROJECT_LAG))
+        handed = ctx.enter_context(tc.tile_pool(name="handed", bufs=3))
+        results = ctx.enter_context(tc.tile_pool(name="results", bufs=4))
+        t_psum = ctx.enter_context(tc.psum_pool(name="t_psum", bufs=2))
+        q_psum = ctx.enter_context(tc.psum_pool(name="q_psum", bufs=ROW_TILES))
+        s_psum = ctx.enter_context(tc.psum_pool(name="s_psum", bufs=PAIR))
+        ctx.enter_context(tc.manual_schedule())
+
+        x_rows, k_rows = {}, {}
+        x_grouped, k_grouped, q_grouped = {}, {}, {}
+        x_mx, k_mx, q_mx = {}, {}, {}
+        q_banks, scores, neg_max, row_sum, inv_sum, probs = {}, {}, {}, {}, {}, {}
+
+        def quantise(grouped, operand):
+            words = handed.tile([P, COLS], U32, tag=operand + "_words", align_bytes=64)
+            scales = handed.tile([P, COLS], U8, tag=operand + "_scales", align_bytes=64)
+            nc.vector.quantize_mx(out=words[:].bitcast(FP8X4), scales=scales[:], in_=grouped[:])
+            return words, scales
+
+        def multiply(acc, stationary, s_cols, moving, m_cols):
+            nc.tensor.matmul_mx(
+                out=acc,
+                lhsT=stationary[0][:, s_cols].bitcast(FP8X4),
+                lhsT_scale=stationary[1][:, s_cols],
+                rhs=moving[0][:, m_cols].bitcast(FP8X4),
+                rhs_scale=moving[1][:, m_cols],
+                start=True,
+                stop=True,
+            )
+
+
+        def load(i):
+            batches = slice(PAIR * i, PAIR * (i + 1))
+            x_tile = rows.tile([P, PAIR, PACK, TOKENS], BF16)
+            for b in range(PAIR):
+                nc.sync.dma_start(
+                    out=x_tile[:, b].rearrange("p j n -> p (j n)"),
+                    in_=x[PAIR * i + b].rearrange("(p j) h w -> p (j h w)", j=PACK),
+                )
+            k_tile = rows.tile([P, ROW_TILES * CHANNELS], BF16)
+            nc.sync.dma_start(
+                out=k_tile[:].rearrange("r (g c) -> r g c", g=ROW_TILES),
+                in_=k[batches].rearrange("b (h r) c -> r (b h) c", r=P),
+            )
+            x_rows[i], k_rows[i] = x_tile, k_tile
+
+        def regroup_x(i):
+            x_side = handed.tile([P, COLS * PACK], BF16, align_bytes=64)
+            by_batch = x_side[:].rearrange("p (b c i j) -> p b c j i", b=PAIR, i=RUN, j=PACK)
+            for b in range(PAIR):
+                nc.scalar.copy(
+                    out=by_batch[:, b], in_=x_rows[i][:, b].rearrange("p j (c i) -> p c j i", i=RUN)
+                )
+            x_grouped[i] = x_side
+
+        def transpose_k(i):
+            k_words = k_rows[i][:].bitcast(F32).rearrange(
+                "r (g w v) -> r g v w", g=ROW_TILES, v=2
+            )
+            k_side = handed.tile([P, COLS * PACK], BF16, align_bytes=64)
+            k_pairs = k_side[:].bitcast(F32).rearrange("p (b h r u) -> p b h r u", b=PAIR, h=HALVES, u=2)
+            banks = []
+            for b in range(PAIR):
+                bank = t_psum.tile([P, HALVES, 2, P], F32)
+                for h in range(HALVES):
+                    for u in range(2):
+                        nc.tensor.transpose(
+                            out=bank[:, h, u, :],
+                            in_=k_words[:, b * HALVES + h, u, :],
+                            identity=ident[:],
+                        )
+                banks.append(bank)
+            for b in range(PAIR):
+                nc.scalar.copy(out=k_pairs[:, b], in_=banks[b][:].rearrange("p h u r -> p h r u"))
+            k_grouped[i] = k_side
+
+        def project(i):
+            q_banks[i] = []
+            for g in range(ROW_TILES):
+                bank = q_psum.tile([P, PACK, P], F32)
+                for t in range(PACK):
+                    multiply(
+                        bank[:, t, :], w_mx, slice(t * P, (t + 1) * P), x_mx[i], slice(g * P, (g + 1) * P)
+                    )
+                q_banks[i].append(bank)
+
+        def q_out_of_psum(i):
+            q_side = handed.tile([P, COLS * PACK], BF16, align_bytes=64)
+            by_tile = q_side[:].rearrange("p (g n t) -> p g n t", g=ROW_TILES, t=PACK)
+            for g in range(ROW_TILES):
+                nc.vector.scalar_tensor_tensor(
+                    out=by_tile[:, g],
+                    in0=q_banks[i][g][:].rearrange("p t n -> p n t"),
+                    scalar=Q_SCALE,
+                    in1=bias_scaled[:].unsqueeze(1).to_broadcast([P, P, PACK]),
+                    op0=ALU.mult,
+                    op1=ALU.add,
+                )
+            q_grouped[i] = q_side
+
+        def score(i):
+            scores[i] = []
+            for b in range(PAIR):
+                bank = s_psum.tile([P, HALVES, KEYS], F32)
+                for h in range(HALVES):
+                    first = b * TOKENS + h * P
+                    multiply(
+                        bank[:, h, :],
+                        q_mx[i],
+                        slice(first, first + P),
+                        k_mx[i],
+                        slice(b * KEYS, (b + 1) * KEYS),
+                    )
+                scores[i].append(bank)
+
+        def row_maxima(i):
+            maxima = handed.tile([P, PAIR, HALVES], F32)
+            for b in range(PAIR):
+                nc.vector.tensor_reduce(
+                    out=maxima[:, b, :],
+                    in_=scores[i][b][:],
+                    axis=mybir.AxisListType.X,
+                    op=ALU.max,
+                    negate=True,
+                )
+            neg_max[i] = maxima
+
+        def exponentials(i):
+            e = results.tile([P, PAIR, HALVES, KEYS], F32)
+            sums = results.tile([P, PAIR, HALVES], F32)
+            for b in range(PAIR):
+                for h in range(HALVES):
+                    nc.scalar.activation(
+                        out=e[:, b, h, :],
+                        in_=scores[i][b][:, h, :],
+                        func=ACT.Exp,
+                        bias=neg_max[i][:, b, h : h + 1],
+                        scale=1.0,
+                        accum_out=sums[:, b, h : h + 1],
+                    )
+            probs[i], row_sum[i] = e, sums
+
+        def invert_sums(i):
+            inverse = results.tile([P, PAIR, HALVES], F32)
+            nc.vector.reciprocal(out=inverse[:], in_=row_sum[i][:])
+            inv_sum[i] = inverse
+
+        def normalise_and_store(i):
+            engine = nc.vector if i == STEPS - 1 else nc.gpsimd
+            for b in range(PAIR):
+                for h in range(HALVES):
+                    engine.tensor_scalar(
+                        out=probs[i][:, b, h, :],
+                        in0=probs[i][:, b, h, :],
+                        scalar1=inv_sum[i][:, b, h : h + 1],
+                        scalar2=0.0,
+                        op0=ALU.mult,
+                        op1=ALU.add,
+                    )
+                nc.sync.dma_start(
+                    out=out[PAIR * i + b].rearrange("(h r) m -> r h m", r=P), in_=probs[i][:, b]
+                )
+
+
+        w_rows = const.tile([P, PACK * CHANNELS], BF16)
+        for u in range(2):
+            nc.sync.dma_start(
+                out=w_rows[:].rearrange("r (u ec) -> r u ec", u=2)[:, u],
+                in_=Wq.rearrange("(r u e) c -> u r (e c)", u=2, e=2)[u],
+            )
+        for i in range(LOOKAHEAD):
+            load(i)
+        bias_bf = const.tile([P, PACK], BF16)
+        nc.scalar.dma_start(
+            out=bias_bf[:],
+            in_=bq.rearrange("(r t) -> r t", t=PACK),
+        )
+
+        warm = const.tile([P, 1], F32)
+        nc.vector.memset(warm[:], 0.0)
+        nc.scalar.activation(out=warm[:], in_=warm[:], func=ACT.Exp)
+
+        ident = const.tile([P, P], F32)
+        make_identity(nc, ident[:])
+
+        bias_scaled = const.tile([P, PACK], F32)
+        nc.vector.tensor_scalar(
+            out=bias_scaled[:], in0=bias_bf[:], scalar1=Q_SCALE, scalar2=None, op0=ALU.mult
+        )
+
+        w_words = w_rows[:].bitcast(F32).rearrange("r (t p v) -> r t v p", t=PACK, v=2)
+        w_side = const.tile([P, PACK * P * PACK], BF16, align_bytes=64)
+        w_pairs = w_side[:].bitcast(F32).rearrange("p (t r v) -> p t r v", t=PACK, v=2)
+        w_banks = []
+        for half in range(2):
+            bank = t_psum.tile([P, 2, 2, P], F32)
+            for t in range(2):
+                for v in range(2):
+                    nc.tensor.transpose(
+                        out=bank[:, t, v, :], in_=w_words[:, 2 * half + t, v, :], identity=ident[:]
+                    )
+            w_banks.append(bank)
+        for half in range(2):
+            nc.vector.tensor_copy(
+                out=w_pairs[:, 2 * half : 2 * half + 2, :, :],
+                in_=w_banks[half][:].rearrange("p t v r -> p t r v"),
+            )
+        w_words_mx = const.tile([P, CHANNELS], U32, align_bytes=64)
+        w_scales = const.tile([P, CHANNELS], U8, align_bytes=64)
+        nc.vector.quantize_mx(out=w_words_mx[:].bitcast(FP8X4), scales=w_scales[:], in_=w_side[:])
+        w_mx = (w_words_mx, w_scales)
+
+
+        def due(i):
+            return 0 <= i < STEPS
+
+        for turn in range(STEPS + NORM_LAG):
+            if due(turn + LOOKAHEAD):
+                load(turn + LOOKAHEAD)
+            if due(turn - NORM_LAG):
+                invert_sums(turn - NORM_LAG)
+                normalise_and_store(turn - NORM_LAG)
+            if due(turn):
+                regroup_x(turn)
+            if due(turn - PROJECT_LAG):
+                transpose_k(turn - PROJECT_LAG)
+            if due(turn - SCORE_LAG):
+                q_out_of_psum(turn - SCORE_LAG)
+            if due(turn - SOFTMAX_LAG):
+                row_maxima(turn - SOFTMAX_LAG)
+                exponentials(turn - SOFTMAX_LAG)
+            if due(turn - PROJECT_LAG):
+                x_mx[turn - PROJECT_LAG] = quantise(x_grouped[turn - PROJECT_LAG], "x")
+                project(turn - PROJECT_LAG)
+            if due(turn - SCORE_LAG):
+                k_mx[turn - SCORE_LAG] = quantise(k_grouped[turn - SCORE_LAG], "k")
+                q_mx[turn - SCORE_LAG] = quantise(q_grouped[turn - SCORE_LAG], "q")
+                score(turn - SCORE_LAG)

@@ -19,10 +19,6 @@ CHANNELS = P * PACK
 TOKENS = 256
 KEYS = 256
 HALVES = TOKENS // P
-PAIR = 2
-STEPS = BATCHES // PAIR
-COLS = PAIR * TOKENS
-ROW_TILES = PAIR * HALVES
 RUN = 4
 Q_SCALE = 1.0 / math.sqrt(CHANNELS)
 
@@ -30,7 +26,9 @@ PROJECT_LAG = 1
 SCORE_LAG = 2
 SOFTMAX_LAG = 3
 NORM_LAG = 4
-LOOKAHEAD = 3
+LOOKAHEAD = 6
+SHARED = 2
+LAST = 2
 
 FLOPS = 2 * BATCHES * TOKENS * CHANNELS * CHANNELS + 2 * BATCHES * TOKENS * KEYS * CHANNELS
 
@@ -39,22 +37,22 @@ def tile_visionattention_pa_t_kernel(tc, x, Wq, bq, k, out):
     nc = tc.nc
     with ExitStack() as ctx:
         const = ctx.enter_context(tc.tile_pool(name="const", bufs=1))
-        rows = ctx.enter_context(tc.tile_pool(name="rows", bufs=LOOKAHEAD + 1 + PROJECT_LAG))
-        handed = ctx.enter_context(tc.tile_pool(name="handed", bufs=3))
-        results = ctx.enter_context(tc.tile_pool(name="results", bufs=4))
+        rows = ctx.enter_context(tc.tile_pool(name="rows", bufs=LOOKAHEAD + 2))
+        handed = ctx.enter_context(tc.tile_pool(name="handed", bufs=4))
+        results = ctx.enter_context(tc.tile_pool(name="results", bufs=6))
         t_psum = ctx.enter_context(tc.psum_pool(name="t_psum", bufs=2))
-        q_psum = ctx.enter_context(tc.psum_pool(name="q_psum", bufs=ROW_TILES))
-        s_psum = ctx.enter_context(tc.psum_pool(name="s_psum", bufs=PAIR))
+        q_psum = ctx.enter_context(tc.psum_pool(name="q_psum", bufs=2 * HALVES))
+        s_psum = ctx.enter_context(tc.psum_pool(name="s_psum", bufs=2))
         ctx.enter_context(tc.manual_schedule())
 
-        x_rows, k_rows = {}, {}
+        x_rows, k_rows, k_banks = {}, {}, {}
         x_grouped, k_grouped, q_grouped = {}, {}, {}
         x_mx, k_mx, q_mx = {}, {}, {}
         q_banks, scores, neg_max, row_sum, inv_sum, probs = {}, {}, {}, {}, {}, {}
 
         def quantise(grouped, operand):
-            words = handed.tile([P, COLS], U32, tag=operand + "_words", align_bytes=64)
-            scales = handed.tile([P, COLS], U8, tag=operand + "_scales", align_bytes=64)
+            words = handed.tile([P, TOKENS], U32, tag=operand + "_words", align_bytes=64)
+            scales = handed.tile([P, TOKENS], U8, tag=operand + "_scales", align_bytes=64)
             nc.vector.quantize_mx(out=words[:].bitcast(FP8X4), scales=scales[:], in_=grouped[:])
             return words, scales
 
@@ -69,66 +67,73 @@ def tile_visionattention_pa_t_kernel(tc, x, Wq, bq, k, out):
                 stop=True,
             )
 
-
-        def load(i):
-            batches = slice(PAIR * i, PAIR * (i + 1))
-            x_tile = rows.tile([P, PAIR, PACK, TOKENS], BF16)
-            for b in range(PAIR):
-                nc.sync.dma_start(
-                    out=x_tile[:, b].rearrange("p j n -> p (j n)"),
-                    in_=x[PAIR * i + b].rearrange("(p j) h w -> p (j h w)", j=PACK),
-                )
-            k_tile = rows.tile([P, ROW_TILES * CHANNELS], BF16)
+        def load_x(i):
+            x_tile = rows.tile([P, PACK, TOKENS], BF16)
             nc.sync.dma_start(
-                out=k_tile[:].rearrange("r (g c) -> r g c", g=ROW_TILES),
-                in_=k[batches].rearrange("b (h r) c -> r (b h) c", r=P),
+                out=x_tile[:].rearrange("p j n -> p (j n)"),
+                in_=x[i].rearrange("(p j) h w -> p (j h w)", j=PACK),
             )
-            x_rows[i], k_rows[i] = x_tile, k_tile
+            x_rows[i] = x_tile
+
+        def load_k(i):
+            k_tile = rows.tile([P, HALVES * CHANNELS], BF16)
+            nc.sync.dma_start(
+                out=k_tile[:].rearrange("r (g c) -> r g c", g=HALVES),
+                in_=k[i].rearrange("(h r) c -> r h c", r=P),
+            )
+            k_rows[i] = k_tile
 
         def regroup_x(i):
-            x_side = handed.tile([P, COLS * PACK], BF16, align_bytes=64)
-            by_batch = x_side[:].rearrange("p (b c i j) -> p b c j i", b=PAIR, i=RUN, j=PACK)
-            for b in range(PAIR):
-                nc.scalar.copy(
-                    out=by_batch[:, b], in_=x_rows[i][:, b].rearrange("p j (c i) -> p c j i", i=RUN)
-                )
+            x_side = handed.tile([P, TOKENS * PACK], BF16, align_bytes=64)
+            out = x_side[:].rearrange("p (c i j) -> p c j i", i=RUN, j=PACK)
+            in_ = x_rows[i][:].rearrange("p j (c i) -> p c j i", i=RUN)
+            half = TOKENS // RUN // 2
+            if i < SHARED:
+                nc.scalar.copy(out=out[:, :half], in_=in_[:, :half])
+                nc.vector.tensor_copy(out=out[:, half:], in_=in_[:, half:])
+            else:
+                nc.scalar.copy(out=out, in_=in_)
             x_grouped[i] = x_side
 
+        def quantise_x(i):
+            x_mx[i] = quantise(x_grouped[i], "x")
+
+        def quantise_k(i):
+            k_mx[i] = quantise(k_grouped[i], "k")
+
+        def quantise_q(i):
+            q_mx[i] = quantise(q_grouped[i], "q")
+
         def transpose_k(i):
-            k_words = k_rows[i][:].bitcast(F32).rearrange(
-                "r (g w v) -> r g v w", g=ROW_TILES, v=2
+            k_words = k_rows[i][:].bitcast(F32).rearrange("r (h w v) -> r h v w", h=HALVES, v=2)
+            bank = t_psum.tile([P, HALVES, 2, P], F32)
+            for h in range(HALVES):
+                for v in range(2):
+                    nc.tensor.transpose(out=bank[:, h, v, :], in_=k_words[:, h, v, :], identity=ident[:])
+            k_banks[i] = bank
+
+        def k_out_of_psum(i):
+            k_side = handed.tile([P, KEYS * PACK], BF16, align_bytes=64)
+            nc.scalar.copy(
+                out=k_side[:].bitcast(F32).rearrange("p (h r v) -> p h r v", h=HALVES, v=2),
+                in_=k_banks[i][:].rearrange("p h v r -> p h r v"),
             )
-            k_side = handed.tile([P, COLS * PACK], BF16, align_bytes=64)
-            k_pairs = k_side[:].bitcast(F32).rearrange("p (b h r u) -> p b h r u", b=PAIR, h=HALVES, u=2)
-            banks = []
-            for b in range(PAIR):
-                bank = t_psum.tile([P, HALVES, 2, P], F32)
-                for h in range(HALVES):
-                    for u in range(2):
-                        nc.tensor.transpose(
-                            out=bank[:, h, u, :],
-                            in_=k_words[:, b * HALVES + h, u, :],
-                            identity=ident[:],
-                        )
-                banks.append(bank)
-            for b in range(PAIR):
-                nc.scalar.copy(out=k_pairs[:, b], in_=banks[b][:].rearrange("p h u r -> p h r u"))
             k_grouped[i] = k_side
 
         def project(i):
             q_banks[i] = []
-            for g in range(ROW_TILES):
+            for g in range(HALVES):
                 bank = q_psum.tile([P, PACK, P], F32)
                 for t in range(PACK):
                     multiply(
-                        bank[:, t, :], w_mx, slice(t * P, (t + 1) * P), x_mx[i], slice(g * P, (g + 1) * P)
+                        bank[:, t, :], w_mx[t // 2], slice(t % 2 * P, (t % 2 + 1) * P), x_mx[i], slice(g * P, (g + 1) * P)
                     )
                 q_banks[i].append(bank)
 
         def q_out_of_psum(i):
-            q_side = handed.tile([P, COLS * PACK], BF16, align_bytes=64)
-            by_tile = q_side[:].rearrange("p (g n t) -> p g n t", g=ROW_TILES, t=PACK)
-            for g in range(ROW_TILES):
+            q_side = handed.tile([P, TOKENS * PACK], BF16, align_bytes=64)
+            by_tile = q_side[:].rearrange("p (g n t) -> p g n t", g=HALVES, t=PACK)
+            for g in range(HALVES):
                 nc.vector.scalar_tensor_tensor(
                     out=by_tile[:, g],
                     in0=q_banks[i][g][:].rearrange("p t n -> p n t"),
@@ -140,67 +145,49 @@ def tile_visionattention_pa_t_kernel(tc, x, Wq, bq, k, out):
             q_grouped[i] = q_side
 
         def score(i):
-            scores[i] = []
-            for b in range(PAIR):
-                bank = s_psum.tile([P, HALVES, KEYS], F32)
-                for h in range(HALVES):
-                    first = b * TOKENS + h * P
-                    multiply(
-                        bank[:, h, :],
-                        q_mx[i],
-                        slice(first, first + P),
-                        k_mx[i],
-                        slice(b * KEYS, (b + 1) * KEYS),
-                    )
-                scores[i].append(bank)
+            bank = s_psum.tile([P, HALVES, KEYS], F32)
+            for h in range(HALVES):
+                multiply(bank[:, h, :], q_mx[i], slice(h * P, (h + 1) * P), k_mx[i], slice(0, KEYS))
+            scores[i] = bank
 
         def row_maxima(i):
-            maxima = handed.tile([P, PAIR, HALVES], F32)
-            for b in range(PAIR):
-                nc.vector.tensor_reduce(
-                    out=maxima[:, b, :],
-                    in_=scores[i][b][:],
-                    axis=mybir.AxisListType.X,
-                    op=ALU.max,
-                    negate=True,
-                )
+            maxima = handed.tile([P, HALVES], F32)
+            nc.vector.tensor_reduce(
+                out=maxima[:], in_=scores[i][:], axis=mybir.AxisListType.X, op=ALU.max, negate=True
+            )
             neg_max[i] = maxima
 
         def exponentials(i):
-            e = results.tile([P, PAIR, HALVES, KEYS], F32)
-            sums = results.tile([P, PAIR, HALVES], F32)
-            for b in range(PAIR):
-                for h in range(HALVES):
-                    nc.scalar.activation(
-                        out=e[:, b, h, :],
-                        in_=scores[i][b][:, h, :],
-                        func=ACT.Exp,
-                        bias=neg_max[i][:, b, h : h + 1],
-                        scale=1.0,
-                        accum_out=sums[:, b, h : h + 1],
-                    )
+            e = results.tile([P, HALVES, KEYS], F32)
+            sums = results.tile([P, HALVES], F32)
+            for h in range(HALVES):
+                nc.scalar.activation(
+                    out=e[:, h, :],
+                    in_=scores[i][:, h, :],
+                    func=ACT.Exp,
+                    bias=neg_max[i][:, h : h + 1],
+                    scale=1.0,
+                    accum_out=sums[:, h : h + 1],
+                )
             probs[i], row_sum[i] = e, sums
 
         def invert_sums(i):
-            inverse = results.tile([P, PAIR, HALVES], F32)
+            inverse = results.tile([P, HALVES], F32)
             nc.vector.reciprocal(out=inverse[:], in_=row_sum[i][:])
             inv_sum[i] = inverse
 
         def normalise_and_store(i):
-            engine = nc.vector if i == STEPS - 1 else nc.gpsimd
-            for b in range(PAIR):
-                for h in range(HALVES):
-                    engine.tensor_scalar(
-                        out=probs[i][:, b, h, :],
-                        in0=probs[i][:, b, h, :],
-                        scalar1=inv_sum[i][:, b, h : h + 1],
-                        scalar2=0.0,
-                        op0=ALU.mult,
-                        op1=ALU.add,
-                    )
-                nc.sync.dma_start(
-                    out=out[PAIR * i + b].rearrange("(h r) m -> r h m", r=P), in_=probs[i][:, b]
+            engine = nc.gpsimd if i < BATCHES - LAST else nc.vector
+            for h in range(HALVES):
+                engine.tensor_scalar(
+                    out=probs[i][:, h, :],
+                    in0=probs[i][:, h, :],
+                    scalar1=inv_sum[i][:, h : h + 1],
+                    scalar2=0.0,
+                    op0=ALU.mult,
+                    op1=ALU.add,
                 )
+            nc.sync.dma_start(out=out[i].rearrange("(h r) m -> r h m", r=P), in_=probs[i][:])
 
 
         w_rows = const.tile([P, PACK * CHANNELS], BF16)
@@ -209,13 +196,14 @@ def tile_visionattention_pa_t_kernel(tc, x, Wq, bq, k, out):
                 out=w_rows[:].rearrange("r (u ec) -> r u ec", u=2)[:, u],
                 in_=Wq.rearrange("(r u e) c -> u r (e c)", u=2, e=2)[u],
             )
-        for i in range(LOOKAHEAD):
-            load(i)
+        load_x(0)
+        load_x(1)
+        load_k(0)
+        for i in range(2, LOOKAHEAD):
+            load_x(i)
+            load_k(i - 1)
         bias_bf = const.tile([P, PACK], BF16)
-        nc.scalar.dma_start(
-            out=bias_bf[:],
-            in_=bq.rearrange("(r t) -> r t", t=PACK),
-        )
+        nc.scalar.dma_start(out=bias_bf[:], in_=bq.rearrange("(r t) -> r t", t=PACK))
 
         warm = const.tile([P, 1], F32)
         nc.vector.memset(warm[:], 0.0)
@@ -224,56 +212,57 @@ def tile_visionattention_pa_t_kernel(tc, x, Wq, bq, k, out):
         ident = const.tile([P, P], F32)
         make_identity(nc, ident[:])
 
+        w_words = w_rows[:].bitcast(F32).rearrange("r (t p v) -> r t v p", t=PACK, v=2)
+        w_banks, w_mx = [], []
+        for u in range(2):
+            bank = t_psum.tile([P, 2, 2, P], F32)
+            for t in range(2):
+                for v in range(2):
+                    nc.tensor.transpose(out=bank[:, t, v, :], in_=w_words[:, 2 * u + t, v, :], identity=ident[:])
+            w_banks.append(bank)
+        w_sides = []
+        for u in range(2):
+            w_side = const.tile([P, 2 * P * PACK], BF16, align_bytes=64, name="w_side%d" % u)
+            w_out = w_side[:].bitcast(F32).rearrange("p (t r v) -> p t r v", t=2, v=2)
+            w_in = w_banks[u][:].rearrange("p t v r -> p t r v")
+            if u == 0:
+                nc.scalar.copy(out=w_out, in_=w_in)
+            else:
+                nc.vector.tensor_copy(out=w_out, in_=w_in)
+            w_sides.append(w_side)
         bias_scaled = const.tile([P, PACK], F32)
         nc.vector.tensor_scalar(
             out=bias_scaled[:], in0=bias_bf[:], scalar1=Q_SCALE, scalar2=None, op0=ALU.mult
         )
-
-        w_words = w_rows[:].bitcast(F32).rearrange("r (t p v) -> r t v p", t=PACK, v=2)
-        w_side = const.tile([P, PACK * P * PACK], BF16, align_bytes=64)
-        w_pairs = w_side[:].bitcast(F32).rearrange("p (t r v) -> p t r v", t=PACK, v=2)
-        w_banks = []
-        for half in range(2):
-            bank = t_psum.tile([P, 2, 2, P], F32)
-            for t in range(2):
-                for v in range(2):
-                    nc.tensor.transpose(
-                        out=bank[:, t, v, :], in_=w_words[:, 2 * half + t, v, :], identity=ident[:]
-                    )
-            w_banks.append(bank)
-        for half in range(2):
-            nc.vector.tensor_copy(
-                out=w_pairs[:, 2 * half : 2 * half + 2, :, :],
-                in_=w_banks[half][:].rearrange("p t v r -> p t r v"),
-            )
-        w_words_mx = const.tile([P, CHANNELS], U32, align_bytes=64)
-        w_scales = const.tile([P, CHANNELS], U8, align_bytes=64)
-        nc.vector.quantize_mx(out=w_words_mx[:].bitcast(FP8X4), scales=w_scales[:], in_=w_side[:])
-        w_mx = (w_words_mx, w_scales)
+        regroup_x(0)
+        for u in range(2):
+            w_words_mx = const.tile([P, 2 * P], U32, align_bytes=64, name="w_words%d" % u)
+            w_scales = const.tile([P, 2 * P], U8, align_bytes=64, name="w_scales%d" % u)
+            nc.vector.quantize_mx(out=w_words_mx[:].bitcast(FP8X4), scales=w_scales[:], in_=w_sides[u][:])
+            w_mx.append((w_words_mx, w_scales))
 
 
         def due(i):
-            return 0 <= i < STEPS
+            return 0 <= i < BATCHES
 
-        for turn in range(STEPS + NORM_LAG):
-            if due(turn + LOOKAHEAD):
-                load(turn + LOOKAHEAD)
-            if due(turn - NORM_LAG):
-                invert_sums(turn - NORM_LAG)
-                normalise_and_store(turn - NORM_LAG)
-            if due(turn):
-                regroup_x(turn)
-            if due(turn - PROJECT_LAG):
-                transpose_k(turn - PROJECT_LAG)
-            if due(turn - SCORE_LAG):
-                q_out_of_psum(turn - SCORE_LAG)
-            if due(turn - SOFTMAX_LAG):
-                row_maxima(turn - SOFTMAX_LAG)
-                exponentials(turn - SOFTMAX_LAG)
-            if due(turn - PROJECT_LAG):
-                x_mx[turn - PROJECT_LAG] = quantise(x_grouped[turn - PROJECT_LAG], "x")
-                project(turn - PROJECT_LAG)
-            if due(turn - SCORE_LAG):
-                k_mx[turn - SCORE_LAG] = quantise(k_grouped[turn - SCORE_LAG], "k")
-                q_mx[turn - SCORE_LAG] = quantise(q_grouped[turn - SCORE_LAG], "q")
-                score(turn - SCORE_LAG)
+        def run(stage, i):
+            if due(i):
+                stage(i)
+
+        transpose_k(0)
+        for turn in range(1, BATCHES + NORM_LAG):
+            run(load_x, turn + LOOKAHEAD - 1)
+            run(load_k, turn + LOOKAHEAD - 2)
+            run(quantise_x, turn - PROJECT_LAG)
+            run(project, turn - PROJECT_LAG)
+            run(row_maxima, turn - SOFTMAX_LAG)
+            run(invert_sums, turn - NORM_LAG)
+            run(quantise_k, turn - SCORE_LAG)
+            run(quantise_q, turn - SCORE_LAG)
+            run(score, turn - SCORE_LAG)
+            run(transpose_k, turn)
+            run(regroup_x, turn)
+            run(q_out_of_psum, turn - PROJECT_LAG)
+            run(k_out_of_psum, turn - PROJECT_LAG)
+            run(exponentials, turn - SOFTMAX_LAG)
+            run(normalise_and_store, turn - NORM_LAG)

@@ -25,8 +25,8 @@ Q_SCALE = 1.0 / math.sqrt(CHANNELS)
 PROJECT_LAG = 1
 SCORE_LAG = 2
 SOFTMAX_LAG = 3
-NORM_LAG = 4
-LOOKAHEAD = 6
+NORM_LAG = 5
+LOOKAHEAD = 8
 SHARED = 2
 LAST = 2
 
@@ -37,15 +37,16 @@ def tile_visionattention_pa_t_kernel(tc, x, Wq, bq, k, out):
     nc = tc.nc
     with ExitStack() as ctx:
         const = ctx.enter_context(tc.tile_pool(name="const", bufs=1))
-        rows = ctx.enter_context(tc.tile_pool(name="rows", bufs=LOOKAHEAD + 2))
-        handed = ctx.enter_context(tc.tile_pool(name="handed", bufs=4))
+        rows = ctx.enter_context(tc.tile_pool(name="rows", bufs=LOOKAHEAD + 3))
+        handed = ctx.enter_context(tc.tile_pool(name="handed", bufs=6))
         results = ctx.enter_context(tc.tile_pool(name="results", bufs=6))
         t_psum = ctx.enter_context(tc.psum_pool(name="t_psum", bufs=2))
-        q_psum = ctx.enter_context(tc.psum_pool(name="q_psum", bufs=2 * HALVES))
+        q_psum = ctx.enter_context(tc.psum_pool(name="q_psum", bufs=HALVES))
+        x_psum = ctx.enter_context(tc.psum_pool(name="x_psum", bufs=2))
         s_psum = ctx.enter_context(tc.psum_pool(name="s_psum", bufs=2))
         ctx.enter_context(tc.manual_schedule())
 
-        x_rows, k_rows, k_banks = {}, {}, {}
+        x_rows, k_rows, k_banks, x_banks = {}, {}, {}, {}
         x_grouped, k_grouped, q_grouped = {}, {}, {}
         x_mx, k_mx, q_mx = {}, {}, {}
         q_banks, scores, neg_max, row_sum, inv_sum, probs = {}, {}, {}, {}, {}, {}
@@ -83,16 +84,29 @@ def tile_visionattention_pa_t_kernel(tc, x, Wq, bq, k, out):
             )
             k_rows[i] = k_tile
 
+        def pass_x(i):
+            if i < SHARED:
+                return
+            bank = x_psum.tile([P, P * PACK], BF16)
+            nc.tensor.matmul(
+                out=bank[:],
+                lhsT=ident_bf[:],
+                rhs=x_rows[i][:].rearrange("p j n -> p n j")[:, P:, :],
+                start=True,
+                stop=True,
+            )
+            x_banks[i] = bank
+
         def regroup_x(i):
             x_side = handed.tile([P, TOKENS * PACK], BF16, align_bytes=64)
             out = x_side[:].rearrange("p (c i j) -> p c j i", i=RUN, j=PACK)
             in_ = x_rows[i][:].rearrange("p j (c i) -> p c j i", i=RUN)
             half = TOKENS // RUN // 2
+            nc.scalar.copy(out=out[:, :half], in_=in_[:, :half])
             if i < SHARED:
-                nc.scalar.copy(out=out[:, :half], in_=in_[:, :half])
                 nc.vector.tensor_copy(out=out[:, half:], in_=in_[:, half:])
             else:
-                nc.scalar.copy(out=out, in_=in_)
+                nc.scalar.copy(out=x_side[:, P * PACK :], in_=x_banks[i][:])
             x_grouped[i] = x_side
 
         def quantise_x(i):
@@ -211,6 +225,8 @@ def tile_visionattention_pa_t_kernel(tc, x, Wq, bq, k, out):
 
         ident = const.tile([P, P], F32)
         make_identity(nc, ident[:])
+        ident_bf = const.tile([P, P], BF16)
+        make_identity(nc, ident_bf[:])
 
         w_words = w_rows[:].bitcast(F32).rearrange("r (t p v) -> r t v p", t=PACK, v=2)
         w_banks, w_mx = [], []
@@ -250,19 +266,22 @@ def tile_visionattention_pa_t_kernel(tc, x, Wq, bq, k, out):
                 stage(i)
 
         transpose_k(0)
+        regroup_x(1)
+        pass_x(2)
         for turn in range(1, BATCHES + NORM_LAG):
             run(load_x, turn + LOOKAHEAD - 1)
             run(load_k, turn + LOOKAHEAD - 2)
             run(quantise_x, turn - PROJECT_LAG)
             run(project, turn - PROJECT_LAG)
-            run(row_maxima, turn - SOFTMAX_LAG)
-            run(invert_sums, turn - NORM_LAG)
             run(quantise_k, turn - SCORE_LAG)
             run(quantise_q, turn - SCORE_LAG)
             run(score, turn - SCORE_LAG)
             run(transpose_k, turn)
-            run(regroup_x, turn)
+            run(pass_x, turn + 2)
+            run(invert_sums, turn - NORM_LAG)
+            run(row_maxima, turn - SOFTMAX_LAG)
             run(q_out_of_psum, turn - PROJECT_LAG)
             run(k_out_of_psum, turn - PROJECT_LAG)
+            run(regroup_x, turn + 1)
             run(exponentials, turn - SOFTMAX_LAG)
             run(normalise_and_store, turn - NORM_LAG)

@@ -23,9 +23,9 @@ RUN = 4
 Q_SCALE = 1.0 / math.sqrt(CHANNELS)
 
 PROJECT_LAG = 1
-SCORE_LAG = 2
-SOFTMAX_LAG = 3
-NORM_LAG = 5
+SCORE_LAG = 3
+SOFTMAX_LAG = 4
+NORM_LAG = 6
 LOOKAHEAD = 8
 SHARED = 2
 LAST = 2
@@ -49,6 +49,7 @@ def tile_visionattention_pa_t_kernel(tc, x, Wq, bq, k, out):
         x_rows, k_rows, k_banks, x_banks = {}, {}, {}, {}
         x_grouped, k_grouped, q_grouped = {}, {}, {}
         x_mx, k_mx, q_mx = {}, {}, {}
+        q_chunks = {}
         q_banks, scores, neg_max, row_sum, inv_sum, probs = {}, {}, {}, {}, {}, {}
 
         def quantise(grouped, operand):
@@ -144,10 +145,13 @@ def tile_visionattention_pa_t_kernel(tc, x, Wq, bq, k, out):
                     )
                 q_banks[i].append(bank)
 
+        def scalar_tiles(i):
+            return 1 if i % 3 == 2 and i > SHARED else 0
+
         def q_out_of_psum(i):
             q_side = handed.tile([P, TOKENS * PACK], BF16, align_bytes=64)
             by_tile = q_side[:].rearrange("p (g n t) -> p g n t", g=HALVES, t=PACK)
-            for g in range(HALVES):
+            for g in range(HALVES - scalar_tiles(i)):
                 nc.vector.scalar_tensor_tensor(
                     out=by_tile[:, g],
                     in0=q_banks[i][g][:].rearrange("p t n -> p n t"),
@@ -157,6 +161,31 @@ def tile_visionattention_pa_t_kernel(tc, x, Wq, bq, k, out):
                     op1=ALU.add,
                 )
             q_grouped[i] = q_side
+
+        def q_by_scalar(i):
+            for g in range(HALVES - scalar_tiles(i), HALVES):
+                chunks = handed.tile([P, PACK, P], BF16)
+                for t in range(PACK):
+                    nc.scalar.activation(
+                        out=chunks[:, t, :],
+                        in_=q_banks[i][g][:, t, :],
+                        func=ACT.Identity,
+                        bias=bias_scaled[:, t : t + 1],
+                        scale=Q_SCALE,
+                    )
+                q_chunks[i] = chunks
+
+        def interleave_q(i):
+            by_tile = q_grouped[i][:].rearrange("p (g n t) -> p g n t", g=HALVES, t=PACK)
+            for g in range(HALVES - scalar_tiles(i), HALVES):
+                nc.gpsimd.tensor_scalar(
+                    out=by_tile[:, g],
+                    in0=q_chunks[i][:].rearrange("p t n -> p n t"),
+                    scalar1=1.0,
+                    scalar2=0.0,
+                    op0=ALU.mult,
+                    op1=ALU.add,
+                )
 
         def score(i):
             bank = s_psum.tile([P, HALVES, KEYS], F32)
@@ -282,6 +311,8 @@ def tile_visionattention_pa_t_kernel(tc, x, Wq, bq, k, out):
             run(row_maxima, turn - SOFTMAX_LAG)
             run(q_out_of_psum, turn - PROJECT_LAG)
             run(k_out_of_psum, turn - PROJECT_LAG)
+            run(q_by_scalar, turn - PROJECT_LAG)
             run(regroup_x, turn + 1)
             run(exponentials, turn - SOFTMAX_LAG)
             run(normalise_and_store, turn - NORM_LAG)
+            run(interleave_q, turn - PROJECT_LAG)

@@ -303,11 +303,11 @@ def tile_visionattention_pa_t_kernel(tc, x, Wq, bq, k, out):
             run(quantise_x, turn - PROJECT_LAG)
             run(project, turn - PROJECT_LAG)
             run(quantise_k, turn - SCORE_LAG)
+            run(invert_sums, turn - NORM_LAG)
             run(quantise_q, turn - SCORE_LAG)
             run(score, turn - SCORE_LAG)
             run(transpose_k, turn)
             run(pass_x, turn + 2)
-            run(invert_sums, turn - NORM_LAG)
             run(row_maxima, turn - SOFTMAX_LAG)
             run(q_out_of_psum, turn - PROJECT_LAG)
             run(k_out_of_psum, turn - PROJECT_LAG)
@@ -315,4 +315,4 @@ def tile_visionattention_pa_t_kernel(tc, x, Wq, bq, k, out):
             run(regroup_x, turn + 1)
             run(exponentials, turn - SOFTMAX_LAG)
             run(normalise_and_store, turn - NORM_LAG)
-            run(interleave_q, turn - PROJECT_LAG)
+            run(interleave_q, turn - PROJECT_LAG - 1)

@@ -103,6 +103,10 @@ def tile_visionattention_pa_t_kernel(tc, x, Wq, bq, k, out):
             out = x_side[:].rearrange("p (c i j) -> p c j i", i=RUN, j=PACK)
             in_ = x_rows[i][:].rearrange("p j (c i) -> p c j i", i=RUN)
             half = TOKENS // RUN // 2
+            if i == 0:
+                nc.vector.tensor_copy(out=out, in_=in_)
+                x_grouped[i] = x_side
+                return
             nc.scalar.copy(out=out[:, :half], in_=in_[:, :half])
             if i < SHARED:
                 nc.vector.tensor_copy(out=out[:, half:], in_=in_[:, half:])
@@ -187,17 +191,25 @@ def tile_visionattention_pa_t_kernel(tc, x, Wq, bq, k, out):
                     op1=ALU.add,
                 )
 
-        def score(i):
-            bank = s_psum.tile([P, HALVES, KEYS], F32)
+        def score(i, pool=s_psum):
+            bank = pool.tile([P, HALVES, KEYS], F32)
             for h in range(HALVES):
                 multiply(bank[:, h, :], q_mx[i], slice(h * P, (h + 1) * P), k_mx[i], slice(0, KEYS))
             scores[i] = bank
 
+        def parts(i):
+            return [slice(h, h + 1) for h in range(HALVES)] if i == BATCHES - 1 else [slice(0, HALVES)]
+
         def row_maxima(i):
             maxima = handed.tile([P, HALVES], F32)
-            nc.vector.tensor_reduce(
-                out=maxima[:], in_=scores[i][:], axis=mybir.AxisListType.X, op=ALU.max, negate=True
-            )
+            for part in parts(i):
+                nc.vector.tensor_reduce(
+                    out=maxima[:, part],
+                    in_=scores[i][:, part, :],
+                    axis=mybir.AxisListType.X,
+                    op=ALU.max,
+                    negate=True,
+                )
             neg_max[i] = maxima
 
         def exponentials(i):
@@ -216,21 +228,29 @@ def tile_visionattention_pa_t_kernel(tc, x, Wq, bq, k, out):
 
         def invert_sums(i):
             inverse = results.tile([P, HALVES], F32)
-            nc.vector.reciprocal(out=inverse[:], in_=row_sum[i][:])
+            for part in parts(i):
+                nc.vector.reciprocal(out=inverse[:, part], in_=row_sum[i][:, part])
+                if i >= BATCHES - LAST:
+                    normalise(nc.vector, i, inverse, part)
             inv_sum[i] = inverse
 
-        def normalise_and_store(i):
-            engine = nc.gpsimd if i < BATCHES - LAST else nc.vector
-            for h in range(HALVES):
+        def normalise(engine, i, inverse, part):
+            for h in range(part.start, part.stop):
                 engine.tensor_scalar(
                     out=probs[i][:, h, :],
                     in0=probs[i][:, h, :],
-                    scalar1=inv_sum[i][:, h : h + 1],
+                    scalar1=inverse[:, h : h + 1],
                     scalar2=0.0,
                     op0=ALU.mult,
                     op1=ALU.add,
                 )
-            nc.sync.dma_start(out=out[i].rearrange("(h r) m -> r h m", r=P), in_=probs[i][:])
+            nc.sync.dma_start(
+                out=out[i].rearrange("(h r) m -> r h m", r=P)[:, part], in_=probs[i][:, part, :]
+            )
+
+        def normalise_and_store(i):
+            if i < BATCHES - LAST:
+                normalise(nc.gpsimd, i, inv_sum[i], slice(0, HALVES))
 
 
         w_rows = const.tile([P, PACK * CHANNELS], BF16)
@@ -270,10 +290,7 @@ def tile_visionattention_pa_t_kernel(tc, x, Wq, bq, k, out):
             w_side = const.tile([P, 2 * P * PACK], BF16, align_bytes=64, name="w_side%d" % u)
             w_out = w_side[:].bitcast(F32).rearrange("p (t r v) -> p t r v", t=2, v=2)
             w_in = w_banks[u][:].rearrange("p t v r -> p t r v")
-            if u == 0:
-                nc.scalar.copy(out=w_out, in_=w_in)
-            else:
-                nc.vector.tensor_copy(out=w_out, in_=w_in)
+            nc.scalar.copy(out=w_out, in_=w_in)
             w_sides.append(w_side)
         bias_scaled = const.tile([P, PACK], F32)
         nc.vector.tensor_scalar(
@@ -285,6 +302,8 @@ def tile_visionattention_pa_t_kernel(tc, x, Wq, bq, k, out):
             w_scales = const.tile([P, 2 * P], U8, align_bytes=64, name="w_scales%d" % u)
             nc.vector.quantize_mx(out=w_words_mx[:].bitcast(FP8X4), scales=w_scales[:], in_=w_sides[u][:])
             w_mx.append((w_words_mx, w_scales))
+            if u == 0:
+                quantise_x(0)
 
 
         def due(i):
@@ -300,7 +319,6 @@ def tile_visionattention_pa_t_kernel(tc, x, Wq, bq, k, out):
         for turn in range(1, BATCHES + NORM_LAG):
             run(load_x, turn + LOOKAHEAD - 1)
             run(load_k, turn + LOOKAHEAD - 2)
-            run(quantise_x, turn - PROJECT_LAG)
             run(project, turn - PROJECT_LAG)
             run(quantise_k, turn - SCORE_LAG)
             run(invert_sums, turn - NORM_LAG)
@@ -312,7 +330,8 @@ def tile_visionattention_pa_t_kernel(tc, x, Wq, bq, k, out):
             run(q_out_of_psum, turn - PROJECT_LAG)
             run(k_out_of_psum, turn - PROJECT_LAG)
             run(q_by_scalar, turn - PROJECT_LAG)
-            run(regroup_x, turn + 1)
             run(exponentials, turn - SOFTMAX_LAG)
+            run(regroup_x, turn + 1)
             run(normalise_and_store, turn - NORM_LAG)
             run(interleave_q, turn - PROJECT_LAG - 1)
+            run(quantise_x, turn)

@@ -28,6 +28,7 @@ SOFTMAX_LAG = 4
 NORM_LAG = 6
 LOOKAHEAD = 8
 SHARED = 2
+WARM_UP = 5
 LAST = 2
 
 FLOPS = 2 * BATCHES * TOKENS * CHANNELS * CHANNELS + 2 * BATCHES * TOKENS * KEYS * CHANNELS
@@ -260,17 +261,23 @@ def tile_visionattention_pa_t_kernel(tc, x, Wq, bq, k, out):
                 in_=Wq.rearrange("(r u e) c -> u r (e c)", u=2, e=2)[u],
             )
         load_x(0)
+        bias_bf = const.tile([P, PACK], BF16)
+        nc.sync.dma_start(out=bias_bf[:], in_=bq.rearrange("(r t) -> r t", t=PACK))
         load_x(1)
         load_k(0)
         for i in range(2, LOOKAHEAD):
             load_x(i)
             load_k(i - 1)
-        bias_bf = const.tile([P, PACK], BF16)
-        nc.scalar.dma_start(out=bias_bf[:], in_=bq.rearrange("(r t) -> r t", t=PACK))
 
         warm = const.tile([P, 1], F32)
         nc.vector.memset(warm[:], 0.0)
         nc.scalar.activation(out=warm[:], in_=warm[:], func=ACT.Exp)
+
+        zeros = const.tile([P, 4 * P], BF16)
+        nc.vector.memset(zeros[:], 0.0)
+        bank = s_psum.tile([P, 4 * P], F32)
+        for n in range(WARM_UP):
+            nc.tensor.matmul(out=bank[:], lhsT=zeros[:, :P], rhs=zeros[:], start=True, stop=True)
 
         ident = const.tile([P, P], F32)
         make_identity(nc, ident[:])
@@ -292,11 +299,11 @@ def tile_visionattention_pa_t_kernel(tc, x, Wq, bq, k, out):
             w_in = w_banks[u][:].rearrange("p t v r -> p t r v")
             nc.scalar.copy(out=w_out, in_=w_in)
             w_sides.append(w_side)
+        regroup_x(0)
         bias_scaled = const.tile([P, PACK], F32)
         nc.vector.tensor_scalar(
             out=bias_scaled[:], in0=bias_bf[:], scalar1=Q_SCALE, scalar2=None, op0=ALU.mult
         )
-        regroup_x(0)
         for u in range(2):
             w_words_mx = const.tile([P, 2 * P], U32, align_bytes=64, name="w_words%d" % u)
             w_scales = const.tile([P, 2 * P], U8, align_bytes=64, name="w_scales%d" % u)

@@ -151,7 +151,7 @@ def tile_visionattention_pa_t_kernel(tc, x, Wq, bq, k, out):
                 q_banks[i].append(bank)
 
         def scalar_tiles(i):
-            return 1 if i % 3 == 2 and i > SHARED else 0
+            return 1 if i % 5 in (2, 4) and i > SHARED else 0
 
         def q_out_of_psum(i):
             q_side = handed.tile([P, TOKENS * PACK], BF16, align_bytes=64)

import math
from contextlib import ExitStack

import concourse.mybir as mybir
from concourse.masks import make_identity

F32 = mybir.dt.float32
BF16 = mybir.dt.bfloat16
U32 = mybir.dt.uint32
U8 = mybir.dt.uint8
FP8X4 = mybir.dt.float8_e4m3fn_x4
ACT = mybir.ActivationFunctionType
ALU = mybir.AluOpType

P = 128
PACK = 4
BATCHES = 32
CHANNELS = P * PACK
TOKENS = 256
KEYS = 256
HALVES = TOKENS // P
RUN = 4
Q_SCALE = 1.0 / math.sqrt(CHANNELS)

PROJECT_LAG = 1
SCORE_LAG = 3
SOFTMAX_LAG = 4
NORM_LAG = 6
LOOKAHEAD = 8
SHARED = 2
WARM_UP = 5
LAST = 2

FLOPS = 2 * BATCHES * TOKENS * CHANNELS * CHANNELS + 2 * BATCHES * TOKENS * KEYS * CHANNELS


def tile_visionattention_pa_t_kernel(tc, x, Wq, bq, k, out):
    nc = tc.nc
    with ExitStack() as ctx:
        const = ctx.enter_context(tc.tile_pool(name="const", bufs=1))
        rows = ctx.enter_context(tc.tile_pool(name="rows", bufs=LOOKAHEAD + 3))
        handed = ctx.enter_context(tc.tile_pool(name="handed", bufs=6))
        results = ctx.enter_context(tc.tile_pool(name="results", bufs=6))
        t_psum = ctx.enter_context(tc.psum_pool(name="t_psum", bufs=2))
        q_psum = ctx.enter_context(tc.psum_pool(name="q_psum", bufs=HALVES))
        x_psum = ctx.enter_context(tc.psum_pool(name="x_psum", bufs=2))
        s_psum = ctx.enter_context(tc.psum_pool(name="s_psum", bufs=2))
        ctx.enter_context(tc.manual_schedule())

        x_rows, k_rows, k_banks, x_banks = {}, {}, {}, {}
        x_grouped, k_grouped, q_grouped = {}, {}, {}
        x_mx, k_mx, q_mx = {}, {}, {}
        q_chunks = {}
        q_banks, scores, neg_max, row_sum, inv_sum, probs = {}, {}, {}, {}, {}, {}

        def quantise(grouped, operand):
            words = handed.tile([P, TOKENS], U32, tag=operand + "_words", align_bytes=64)
            scales = handed.tile([P, TOKENS], U8, tag=operand + "_scales", align_bytes=64)
            nc.vector.quantize_mx(out=words[:].bitcast(FP8X4), scales=scales[:], in_=grouped[:])
            return words, scales

        def multiply(acc, stationary, s_cols, moving, m_cols):
            nc.tensor.matmul_mx(
                out=acc,
                lhsT=stationary[0][:, s_cols].bitcast(FP8X4),
                lhsT_scale=stationary[1][:, s_cols],
                rhs=moving[0][:, m_cols].bitcast(FP8X4),
                rhs_scale=moving[1][:, m_cols],
                start=True,
                stop=True,
            )

        def load_x(i):
            x_tile = rows.tile([P, PACK, TOKENS], BF16)
            nc.sync.dma_start(
                out=x_tile[:].rearrange("p j n -> p (j n)"),
                in_=x[i].rearrange("(p j) h w -> p (j h w)", j=PACK),
            )
            x_rows[i] = x_tile

        def load_k(i):
            k_tile = rows.tile([P, HALVES * CHANNELS], BF16)
            nc.sync.dma_start(
                out=k_tile[:].rearrange("r (g c) -> r g c", g=HALVES),
                in_=k[i].rearrange("(h r) c -> r h c", r=P),
            )
            k_rows[i] = k_tile

        def pass_x(i):
            if i < SHARED:
                return
            bank = x_psum.tile([P, P * PACK], BF16)
            nc.tensor.matmul(
                out=bank[:],
                lhsT=ident_bf[:],
                rhs=x_rows[i][:].rearrange("p j n -> p n j")[:, P:, :],
                start=True,
                stop=True,
            )
            x_banks[i] = bank

        def regroup_x(i):
            x_side = handed.tile([P, TOKENS * PACK], BF16, align_bytes=64)
            out = x_side[:].rearrange("p (c i j) -> p c j i", i=RUN, j=PACK)
            in_ = x_rows[i][:].rearrange("p j (c i) -> p c j i", i=RUN)
            half = TOKENS // RUN // 2
            if i == 0:
                nc.vector.tensor_copy(out=out, in_=in_)
                x_grouped[i] = x_side
                return
            nc.scalar.copy(out=out[:, :half], in_=in_[:, :half])
            if i < SHARED:
                nc.vector.tensor_copy(out=out[:, half:], in_=in_[:, half:])
            else:
                nc.scalar.copy(out=x_side[:, P * PACK :], in_=x_banks[i][:])
            x_grouped[i] = x_side

        def quantise_x(i):
            x_mx[i] = quantise(x_grouped[i], "x")

        def quantise_k(i):
            k_mx[i] = quantise(k_grouped[i], "k")

        def quantise_q(i):
            q_mx[i] = quantise(q_grouped[i], "q")

        def transpose_k(i):
            k_words = k_rows[i][:].bitcast(F32).rearrange("r (h w v) -> r h v w", h=HALVES, v=2)
            bank = t_psum.tile([P, HALVES, 2, P], F32)
            for h in range(HALVES):
                for v in range(2):
                    nc.tensor.transpose(out=bank[:, h, v, :], in_=k_words[:, h, v, :], identity=ident[:])
            k_banks[i] = bank

        def k_out_of_psum(i):
            k_side = handed.tile([P, KEYS * PACK], BF16, align_bytes=64)
            nc.scalar.copy(
                out=k_side[:].bitcast(F32).rearrange("p (h r v) -> p h r v", h=HALVES, v=2),
                in_=k_banks[i][:].rearrange("p h v r -> p h r v"),
            )
            k_grouped[i] = k_side

        def project(i):
            q_banks[i] = []
            for g in range(HALVES):
                bank = q_psum.tile([P, PACK, P], F32)
                for t in range(PACK):
                    multiply(
                        bank[:, t, :], w_mx[t // 2], slice(t % 2 * P, (t % 2 + 1) * P), x_mx[i], slice(g * P, (g + 1) * P)
                    )
                q_banks[i].append(bank)

        def scalar_tiles(i):
            return 1 if i % 5 in (2, 4) and i > SHARED else 0

        def q_out_of_psum(i):
            q_side = handed.tile([P, TOKENS * PACK], BF16, align_bytes=64)
            by_tile = q_side[:].rearrange("p (g n t) -> p g n t", g=HALVES, t=PACK)
            for g in range(HALVES - scalar_tiles(i)):
                nc.vector.scalar_tensor_tensor(
                    out=by_tile[:, g],
                    in0=q_banks[i][g][:].rearrange("p t n -> p n t"),
                    scalar=Q_SCALE,
                    in1=bias_scaled[:].unsqueeze(1).to_broadcast([P, P, PACK]),
                    op0=ALU.mult,
                    op1=ALU.add,
                )
            q_grouped[i] = q_side

        def q_by_scalar(i):
            for g in range(HALVES - scalar_tiles(i), HALVES):
                chunks = handed.tile([P, PACK, P], BF16)
                for t in range(PACK):
                    nc.scalar.activation(
                        out=chunks[:, t, :],
                        in_=q_banks[i][g][:, t, :],
                        func=ACT.Identity,
                        bias=bias_scaled[:, t : t + 1],
                        scale=Q_SCALE,
                    )
                q_chunks[i] = chunks

        def interleave_q(i):
            by_tile = q_grouped[i][:].rearrange("p (g n t) -> p g n t", g=HALVES, t=PACK)
            for g in range(HALVES - scalar_tiles(i), HALVES):
                nc.gpsimd.tensor_scalar(
                    out=by_tile[:, g],
                    in0=q_chunks[i][:].rearrange("p t n -> p n t"),
                    scalar1=1.0,
                    scalar2=0.0,
                    op0=ALU.mult,
                    op1=ALU.add,
                )

        def score(i, pool=s_psum):
            bank = pool.tile([P, HALVES, KEYS], F32)
            for h in range(HALVES):
                multiply(bank[:, h, :], q_mx[i], slice(h * P, (h + 1) * P), k_mx[i], slice(0, KEYS))
            scores[i] = bank

        def parts(i):
            return [slice(h, h + 1) for h in range(HALVES)] if i == BATCHES - 1 else [slice(0, HALVES)]

        def row_maxima(i):
            maxima = handed.tile([P, HALVES], F32)
            for part in parts(i):
                nc.vector.tensor_reduce(
                    out=maxima[:, part],
                    in_=scores[i][:, part, :],
                    axis=mybir.AxisListType.X,
                    op=ALU.max,
                    negate=True,
                )
            neg_max[i] = maxima

        def exponentials(i):
            e = results.tile([P, HALVES, KEYS], F32)
            sums = results.tile([P, HALVES], F32)
            for h in range(HALVES):
                nc.scalar.activation(
                    out=e[:, h, :],
                    in_=scores[i][:, h, :],
                    func=ACT.Exp,
                    bias=neg_max[i][:, h : h + 1],
                    scale=1.0,
                    accum_out=sums[:, h : h + 1],
                )
            probs[i], row_sum[i] = e, sums

        def invert_sums(i):
            inverse = results.tile([P, HALVES], F32)
            for part in parts(i):
                nc.vector.reciprocal(out=inverse[:, part], in_=row_sum[i][:, part])
                if i >= BATCHES - LAST:
                    normalise(nc.vector, i, inverse, part)
            inv_sum[i] = inverse

        def normalise(engine, i, inverse, part):
            for h in range(part.start, part.stop):
                engine.tensor_scalar(
                    out=probs[i][:, h, :],
                    in0=probs[i][:, h, :],
                    scalar1=inverse[:, h : h + 1],
                    scalar2=0.0,
                    op0=ALU.mult,
                    op1=ALU.add,
                )
            nc.sync.dma_start(
                out=out[i].rearrange("(h r) m -> r h m", r=P)[:, part], in_=probs[i][:, part, :]
            )

        def normalise_and_store(i):
            if i < BATCHES - LAST:
                normalise(nc.gpsimd, i, inv_sum[i], slice(0, HALVES))


        w_rows = const.tile([P, PACK * CHANNELS], BF16)
        for u in range(2):
            nc.sync.dma_start(
                out=w_rows[:].rearrange("r (u ec) -> r u ec", u=2)[:, u],
                in_=Wq.rearrange("(r u e) c -> u r (e c)", u=2, e=2)[u],
            )
        load_x(0)
        bias_bf = const.tile([P, PACK], BF16)
        nc.sync.dma_start(out=bias_bf[:], in_=bq.rearrange("(r t) -> r t", t=PACK))
        load_x(1)
        load_k(0)
        for i in range(2, LOOKAHEAD):
            load_x(i)
            load_k(i - 1)

        warm = const.tile([P, 1], F32)
        nc.vector.memset(warm[:], 0.0)
        nc.scalar.activation(out=warm[:], in_=warm[:], func=ACT.Exp)

        zeros = const.tile([P, 4 * P], BF16)
        nc.vector.memset(zeros[:], 0.0)
        bank = s_psum.tile([P, 4 * P], F32)
        for n in range(WARM_UP):
            nc.tensor.matmul(out=bank[:], lhsT=zeros[:, :P], rhs=zeros[:], start=True, stop=True)

        ident = const.tile([P, P], F32)
        make_identity(nc, ident[:])
        ident_bf = const.tile([P, P], BF16)
        make_identity(nc, ident_bf[:])

        w_words = w_rows[:].bitcast(F32).rearrange("r (t p v) -> r t v p", t=PACK, v=2)
        w_banks, w_mx = [], []
        for u in range(2):
            bank = t_psum.tile([P, 2, 2, P], F32)
            for t in range(2):
                for v in range(2):
                    nc.tensor.transpose(out=bank[:, t, v, :], in_=w_words[:, 2 * u + t, v, :], identity=ident[:])
            w_banks.append(bank)
        w_sides = []
        for u in range(2):
            w_side = const.tile([P, 2 * P * PACK], BF16, align_bytes=64, name="w_side%d" % u)
            w_out = w_side[:].bitcast(F32).rearrange("p (t r v) -> p t r v", t=2, v=2)
            w_in = w_banks[u][:].rearrange("p t v r -> p t r v")
            nc.scalar.copy(out=w_out, in_=w_in)
            w_sides.append(w_side)
        regroup_x(0)
        bias_scaled = const.tile([P, PACK], F32)
        nc.vector.tensor_scalar(
            out=bias_scaled[:], in0=bias_bf[:], scalar1=Q_SCALE, scalar2=None, op0=ALU.mult
        )
        for u in range(2):
            w_words_mx = const.tile([P, 2 * P], U32, align_bytes=64, name="w_words%d" % u)
            w_scales = const.tile([P, 2 * P], U8, align_bytes=64, name="w_scales%d" % u)
            nc.vector.quantize_mx(out=w_words_mx[:].bitcast(FP8X4), scales=w_scales[:], in_=w_sides[u][:])
            w_mx.append((w_words_mx, w_scales))
            if u == 0:
                quantise_x(0)


        def due(i):
            return 0 <= i < BATCHES

        def run(stage, i):
            if due(i):
                stage(i)

        transpose_k(0)
        regroup_x(1)
        pass_x(2)
        for turn in range(1, BATCHES + NORM_LAG):
            run(load_x, turn + LOOKAHEAD - 1)
            run(load_k, turn + LOOKAHEAD - 2)
            run(project, turn - PROJECT_LAG)
            run(quantise_k, turn - SCORE_LAG)
            run(invert_sums, turn - NORM_LAG)
            run(quantise_q, turn - SCORE_LAG)
            run(score, turn - SCORE_LAG)
            run(transpose_k, turn)
            run(pass_x, turn + 2)
            run(row_maxima, turn - SOFTMAX_LAG)
            run(q_out_of_psum, turn - PROJECT_LAG)
            run(k_out_of_psum, turn - PROJECT_LAG)
            run(q_by_scalar, turn - PROJECT_LAG)
            run(exponentials, turn - SOFTMAX_LAG)
            run(regroup_x, turn + 1)
            run(normalise_and_store, turn - NORM_LAG)
            run(interleave_q, turn - PROJECT_LAG - 1)
            run(quantise_x, turn)
